import numpy as np
import ml_dtypes


def mxq(x, axis, fmt="e4m3"):
    dtype, down = {"e4m3": (ml_dtypes.float8_e4m3fn, 7), "e5m2": (ml_dtypes.float8_e5m2, 14)}[fmt]
    v = np.moveaxis(np.asarray(x, np.float32).astype(ml_dtypes.bfloat16).astype(np.float64), axis, -1)
    blocks = v.reshape(v.shape[:-1] + (-1, 32))
    amax = np.abs(blocks).max(-1, keepdims=True)
    byte = np.maximum(np.where(amax > 0, np.frexp(amax)[1] - 1 + 127, 0) - down, 1)
    scale = np.exp2(byte - 127.0)
    codes = (blocks / scale).astype(np.float32).astype(dtype).astype(np.float64)
    return np.moveaxis((codes * scale).reshape(v.shape), -1, axis)


WIDE = False


def mx_kscale(k):
    if not WIDE:
        return np.ones(k)
    levels = np.array([20, -20, 10, -10, 0])
    a = np.random.permutation(np.resize(levels, k // 512 * 4)).reshape(k // 512, 4)
    idx = np.arange(k)
    return np.exp2(a[idx // 512, idx % 128 // 32])


BF16 = ml_dtypes.bfloat16


def bf(x):
    return np.asarray(x, np.float32).astype(BF16)


def f64(x):
    return np.asarray(x).astype(np.float64)


B, C, S, OUT = 1024, 4, 32, 512
IN = C * S * S
HS = S // 2


def haar_dwt2_features(x):
    x4 = x.reshape(x.shape[0], C, S, S)
    a = x4[:, :, 0::2, 0::2]
    bq = x4[:, :, 0::2, 1::2]
    c = x4[:, :, 1::2, 0::2]
    d = x4[:, :, 1::2, 1::2]
    LL = (a + bq + c + d) * 0.5
    LH = (a + bq - c - d) * 0.5
    HL = (a - bq + c - d) * 0.5
    HH = (a - bq - c + d) * 0.5
    t = np.stack([LL, LH, HL, HH], axis=2)
    return t.reshape(x.shape[0], -1)


def setup_inputs():
    s = mx_kscale(B)[:, None]
    x = np.random.standard_normal((B, IN)) * s
    W = np.random.standard_normal((OUT, IN)) * (1.0 / np.sqrt(IN))
    b = np.random.standard_normal(OUT) * 0.5
    g = np.random.standard_normal((B, OUT)) * np.exp2(np.random.randint(-12, 1, (B, 1))) / s
    return {"x": bf(x), "W": bf(W), "b": bf(b), "grad_out": bf(g)}


def reference(x, W, b, grad_out):
    t = haar_dwt2_features(f64(x))
    return mxq(f64(grad_out), 0, "e5m2").T @ mxq(t, 0, "e4m3")

@@ -1,0 +1,205 @@
+from contextlib import ExitStack
+
+import concourse.mybir as mybir
+from concourse.masks import make_identity
+
+FLOPS = 2 * 512 * 1024 * 4096
+BYTES = 1024 * 4096 * 2 + 1024 * 512 * 2 + 512 * 4096 * 4
+
+MANUAL = False
+
+BF16 = mybir.dt.bfloat16
+F32 = mybir.dt.float32
+U32 = mybir.dt.uint32
+U8 = mybir.dt.uint8
+E4X4 = mybir.dt.float8_e4m3fn_x4
+E5X4 = mybir.dt.float8_e5m2_x4
+ADD = mybir.AluOpType.add
+SUB = mybir.AluOpType.subtract
+COPY = mybir.ActivationFunctionType.Copy
+
+P = 128
+PE_UNITS = 3
+V_I = 16 - 2 * PE_UNITS
+V_Q = V_I * 32
+
+
+def tile_waveletlinearlayer_kernel(tc, x, W, b, grad_out, out):
+    nc = tc.nc
+    xv = x.rearrange("(c p j) f -> c p j f", c=2, p=P, j=4)
+    gv = grad_out.rearrange("(c p j) m -> p c j m", c=2, p=P, j=4)
+    with ExitStack() as ctx:
+        const = ctx.enter_context(tc.tile_pool(name="const", bufs=1))
+        xpool = ctx.enter_context(tc.tile_pool(name="xpool", bufs=8))
+        spool = ctx.enter_context(tc.tile_pool(name="spool", bufs=2))
+        gpool = ctx.enter_context(tc.tile_pool(name="gpool", bufs=3))
+        tpool = ctx.enter_context(tc.tile_pool(name="tpool", bufs=4))
+        xtpool = ctx.enter_context(tc.tile_pool(name="xtpool", bufs=3))
+        opool = ctx.enter_context(tc.tile_pool(name="opool", bufs=8))
+        ps_xt = ctx.enter_context(tc.psum_pool(name="ps_xt", bufs=2))
+        ps_hm = ctx.enter_context(tc.psum_pool(name="ps_hm", bufs=2))
+        ps_acc = ctx.enter_context(tc.psum_pool(name="ps_acc", bufs=4))
+        if MANUAL:
+            ctx.enter_context(tc.manual_schedule())
+
+        xs = []
+        for k in range(8):
+            xk = xpool.tile([P, 4, 512, 2], BF16, name="xk", tag="xk")
+            xs.append(xk)
+        g_raw = const.tile([P, 2, 4, 512], BF16, name="g_raw")
+
+        def load_x(k, f0, f1):
+            c = k % 2
+            ch = k // 2
+            nc.sync.dma_start(
+                out=xs[k].rearrange("p j q e -> p j (q e)")[:, :, f0:f1],
+                in_=xv[c][:, :, ch * 1024 + f0 : ch * 1024 + f1],
+            )
+
+        load_x(0, 0, 2 * V_Q)
+        load_x(0, 2 * V_Q, 1024)
+        load_x(1, 0, 1024)
+        nc.sync.dma_start(out=g_raw[:], in_=gv)
+        for k in range(2, 8):
+            load_x(k, 0, 1024)
+
+        ident = const.tile([P, P], BF16, name="ident")
+        make_identity(nc, ident[:])
+        hs = const.tile([P, 2, 2, 2, 16], BF16, name="hs")
+        hmat = const.tile([P, 2, 2, 2, 16], BF16, name="hmat")
+        idv = ident.rearrange("p (q e) -> p q e", e=2)
+        for pl, op in ((0, ADD), (1, SUB)):
+            nc.vector.tensor_tensor(
+                out=hs[:, pl].rearrange("p a r c -> p (a r c)"),
+                in0=idv[:, :, 0],
+                in1=idv[:, :, 1],
+                op=op,
+            )
+        for s2, op in ((0, ADD), (1, SUB)):
+            nc.vector.tensor_tensor(
+                out=hmat[:, :, s2], in0=hs[:, :, :, 0, :], in1=hs[:, :, :, 1, :], op=op
+            )
+        hflat = hmat.rearrange("p a b c d -> p (a b c d)")
+
+        gg = const.tile([P, 2, 512, 4], BF16, name="gg", align_bytes=64)
+        gc = const.tile([P, 2, 512], U32, name="gc", align_bytes=64)
+        gs = const.tile([P, 2, 512], U8, name="gs", align_bytes=64)
+
+        grouped = {}
+        codes = {}
+
+        def pe_transposes(k, u):
+            xtp = ps_xt.tile([P, 4, P], BF16, name="xtp", tag="xtp")
+            q0 = V_Q + 64 * u
+            for j in range(4):
+                nc.tensor.transpose(
+                    xtp[:, j, :],
+                    xs[k][:, j, q0 : q0 + 64, :].rearrange("p q e -> p (q e)"),
+                    ident[:],
+                )
+            xt = xtpool.tile([P, 4, P], BF16, name="xt", tag="xt")
+            nc.scalar.copy(out=xt[:], in_=xtp[:])
+            return xt
+
+        def pe_matmuls(k, u, xt):
+            hm = ps_hm.tile([P, 4, P], F32, name="hm", tag="hm")
+            for j in range(4):
+                nc.tensor.matmul(hm[:, j, :], lhsT=xt[:, j, :], rhs=hflat, start=True, stop=True)
+            w0 = (V_I + 2 * u) * 64
+            nc.scalar.copy(
+                out=grouped[k]
+                .rearrange("p a b i w -> p (a b) (i w)")[:, :, w0 : w0 + 128]
+                .rearrange("p s (w j) -> p s w j", j=4),
+                in_=hm.rearrange("p j (s w) -> p s w j", s=4),
+            )
+
+        def pe_path(k):
+            gk = gpool.tile([P, 2, 2, 16, 64], BF16, name="gk", tag="gk", align_bytes=64)
+            grouped[k] = gk
+            xt0 = pe_transposes(k, 0)
+            xt1 = pe_transposes(k, 1)
+            pe_matmuls(k, 0, xt0)
+            xt2 = pe_transposes(k, 2)
+            pe_matmuls(k, 1, xt1)
+            pe_matmuls(k, 2, xt2)
+
+        stage1 = {}
+
+        def st1(k):
+            sk = spool.tile([P, 2, V_I, 2, 64], F32, name="sk", tag="sk")
+            stage1[k] = sk
+            for pl, op in ((0, ADD), (1, SUB)):
+                nc.vector.tensor_tensor(
+                    out=sk[:, pl].rearrange("p i r (c j) -> p (i r c) j", j=4),
+                    in0=xs[k][:, :, 0:V_Q, 0].rearrange("p j q -> p q j"),
+                    in1=xs[k][:, :, 0:V_Q, 1].rearrange("p j q -> p q j"),
+                    op=op,
+                )
+
+        def st2(k):
+            sk = stage1[k]
+            for s2, op in ((0, ADD), (1, SUB)):
+                nc.vector.tensor_tensor(
+                    out=grouped[k][:, :, s2, 0:V_I, :],
+                    in0=sk[:, :, :, 0, :],
+                    in1=sk[:, :, :, 1, :],
+                    op=op,
+                )
+
+        def quant(k):
+            tck = tpool.tile([P, 1024], U32, name="tck", tag="tck", align_bytes=64)
+            tsk = tpool.tile([P, 1024], U8, name="tsk", tag="tsk", align_bytes=64)
+            codes[k] = (tck, tsk)
+            nc.vector.quantize_mx(
+                out=tck[:].bitcast(E4X4),
+                scales=tsk[:],
+                in_=grouped[k].rearrange("p a b i w -> p (a b i w)"),
+            )
+
+        def mx(ch, share):
+            for n2 in range(2):
+                cols = slice(n2 * 512, n2 * 512 + 512)
+                for m in range(4):
+                    rows = slice(m * P, m * P + P)
+                    acc = ps_acc.tile([P, 512], F32, name="acc", tag="acc")
+                    for c in range(2):
+                        tck, tsk = codes[2 * ch + c]
+                        nc.tensor.matmul_mx(
+                            out=acc[:],
+                            lhsT=gc[:, c, rows].bitcast(E5X4),
+                            lhsT_scale=gs[:, c, rows],
+                            rhs=tck[:, cols].bitcast(E4X4),
+                            rhs_scale=tsk[:, cols],
+                            start=(c == 0),
+                            stop=(c == 1),
+                        )
+                    o = opool.tile([P, 512], F32, name="o", tag="o")
+                    if share and m % 2 == 1:
+                        nc.vector.tensor_scalar_mul(out=o[:], in0=acc[:], scalar1=0.5)
+                    else:
+                        nc.scalar.activation(out=o[:], in_=acc[:], func=COPY, scale=0.5)
+                    nc.sync.dma_start(
+                        out=out[rows, ch * 1024 + n2 * 512 : ch * 1024 + n2 * 512 + 512], in_=o[:]
+                    )
+
+        pe_path(0)
+        pe_path(1)
+        for c in range(2):
+            nc.scalar.copy(out=gg[:, c], in_=g_raw[:, c].rearrange("p j m -> p m j"))
+        for k in range(8):
+            st1(k)
+            if k >= 1:
+                quant(k - 1)
+            if k == 1:
+                nc.vector.quantize_mx(
+                    out=gc.rearrange("p c m -> p (c m)").bitcast(E5X4),
+                    scales=gs.rearrange("p c m -> p (c m)"),
+                    in_=gg.rearrange("p c m j -> p (c m j)"),
+                )
+            if k >= 2 and k % 2 == 0:
+                mx(k // 2 - 1, False)
+            st2(k)
+            if k + 2 < 8:
+                pe_path(k + 2)
+        quant(7)
+        mx(3, True)

@@ -130,21 +130,24 @@ def tile_waveletlinearlayer_kernel(tc, x, W, b, grad_out, out):
             stage1[k] = sk
             for pl, op in ((0, ADD), (1, SUB)):
                 nc.vector.tensor_tensor(
-                    out=sk[:, pl].rearrange("p i r (c j) -> p (i r c) j", j=4),
-                    in0=xs[k][:, :, 0:V_Q, 0].rearrange("p j q -> p q j"),
-                    in1=xs[k][:, :, 0:V_Q, 1].rearrange("p j q -> p q j"),
+                    out=sk[:, pl].rearrange("p i r (c j e) -> p (i r c) j e", j=4, e=4),
+                    in0=xs[k][:, :, 0:V_Q, 0].rearrange("p j (c e) -> p c j e", e=4),
+                    in1=xs[k][:, :, 0:V_Q, 1].rearrange("p j (c e) -> p c j e", e=4),
                     op=op,
                 )
 
         def st2(k):
             sk = stage1[k]
-            for s2, op in ((0, ADD), (1, SUB)):
-                nc.vector.tensor_tensor(
-                    out=grouped[k][:, :, s2, 0:V_I, :],
-                    in0=sk[:, :, :, 0, :],
-                    in1=sk[:, :, :, 1, :],
-                    op=op,
-                )
+            for pl in range(2):
+                for s2, op in ((0, ADD), (1, SUB)):
+                    nc.vector.tensor_tensor(
+                        out=grouped[k][:, pl, s2, 0:V_I, :].rearrange(
+                            "p i (c e j) -> p i c j e", c=4, e=4, j=4
+                        ),
+                        in0=sk[:, pl, :, 0, :].rearrange("p i (c j e) -> p i c j e", c=4, j=4, e=4),
+                        in1=sk[:, pl, :, 1, :].rearrange("p i (c j e) -> p i c j e", c=4, j=4, e=4),
+                        op=op,
+                    )
 
         def quant(k):
             tck = tpool.tile([P, 1024], U32, name="tck", tag="tck", align_bytes=64)

@@ -6,7 +6,7 @@ from concourse.masks import make_identity
 FLOPS = 2 * 512 * 1024 * 4096
 BYTES = 1024 * 4096 * 2 + 1024 * 512 * 2 + 512 * 4096 * 4
 
-MANUAL = False
+MANUAL = True
 
 BF16 = mybir.dt.bfloat16
 F32 = mybir.dt.float32
@@ -22,6 +22,7 @@ P = 128
 PE_UNITS = 3
 V_I = 16 - 2 * PE_UNITS
 V_Q = V_I * 32
+HEAD = ((0, 2), (2, 5), (5, V_I))
 
 
 def tile_waveletlinearlayer_kernel(tc, x, W, b, grad_out, out):
@@ -56,7 +57,8 @@ def tile_waveletlinearlayer_kernel(tc, x, W, b, grad_out, out):
                 in_=xv[c][:, :, ch * 1024 + f0 : ch * 1024 + f1],
             )
 
-        load_x(0, 0, 2 * V_Q)
+        for i0, i1 in HEAD:
+            load_x(0, 64 * i0, 64 * i1)
         load_x(0, 2 * V_Q, 1024)
         load_x(1, 0, 1024)
         nc.sync.dma_start(out=g_raw[:], in_=gv)
@@ -125,84 +127,126 @@ def tile_waveletlinearlayer_kernel(tc, x, W, b, grad_out, out):
 
         stage1 = {}
 
-        def st1(k):
+        def st1(k, pieces):
             sk = spool.tile([P, 2, V_I, 2, 64], F32, name="sk", tag="sk")
             stage1[k] = sk
-            for pl, op in ((0, ADD), (1, SUB)):
-                nc.vector.tensor_tensor(
-                    out=sk[:, pl].rearrange("p i r (c j e) -> p (i r c) j e", j=4, e=4),
-                    in0=xs[k][:, :, 0:V_Q, 0].rearrange("p j (c e) -> p c j e", e=4),
-                    in1=xs[k][:, :, 0:V_Q, 1].rearrange("p j (c e) -> p c j e", e=4),
-                    op=op,
-                )
-
-        def st2(k):
-            sk = stage1[k]
-            for pl in range(2):
-                for s2, op in ((0, ADD), (1, SUB)):
+            for i0, i1 in pieces:
+                for pl, op in ((0, ADD), (1, SUB)):
                     nc.vector.tensor_tensor(
-                        out=grouped[k][:, pl, s2, 0:V_I, :].rearrange(
-                            "p i (c e j) -> p i c j e", c=4, e=4, j=4
-                        ),
-                        in0=sk[:, pl, :, 0, :].rearrange("p i (c j e) -> p i c j e", c=4, j=4, e=4),
-                        in1=sk[:, pl, :, 1, :].rearrange("p i (c j e) -> p i c j e", c=4, j=4, e=4),
+                        out=sk[:, pl, i0:i1].rearrange("p i r (c j e) -> p (i r c) j e", j=4, e=4),
+                        in0=xs[k][:, :, 32 * i0 : 32 * i1, 0].rearrange("p j (c e) -> p c j e", e=4),
+                        in1=xs[k][:, :, 32 * i0 : 32 * i1, 1].rearrange("p j (c e) -> p c j e", e=4),
                         op=op,
                     )
 
-        def quant(k):
+        def st2_one(k, pl, s2):
+            sk = stage1[k]
+            nc.vector.tensor_tensor(
+                out=grouped[k][:, pl, s2, 0:V_I, :].rearrange(
+                    "p i (c e j) -> p i c j e", c=4, e=4, j=4
+                ),
+                in0=sk[:, pl, :, 0, :].rearrange("p i (c j e) -> p i c j e", c=4, j=4, e=4),
+                in1=sk[:, pl, :, 1, :].rearrange("p i (c j e) -> p i c j e", c=4, j=4, e=4),
+                op=(ADD, SUB)[s2],
+            )
+
+        def st2(k):
+            for pl in range(2):
+                for s2 in range(2):
+                    st2_one(k, pl, s2)
+
+        def new_codes(k):
             tck = tpool.tile([P, 1024], U32, name="tck", tag="tck", align_bytes=64)
             tsk = tpool.tile([P, 1024], U8, name="tsk", tag="tsk", align_bytes=64)
             codes[k] = (tck, tsk)
+
+        def quant(k, w0, w1):
+            tck, tsk = codes[k]
             nc.vector.quantize_mx(
-                out=tck[:].bitcast(E4X4),
-                scales=tsk[:],
-                in_=grouped[k].rearrange("p a b i w -> p (a b i w)"),
+                out=tck[:, w0:w1].bitcast(E4X4),
+                scales=tsk[:, w0:w1],
+                in_=grouped[k].rearrange("p a b i w -> p (a b i w)")[:, 4 * w0 : 4 * w1],
             )
 
-        def mx(ch, share):
+        def mx_pass(acc, ch, n2, m, c):
+            tck, tsk = codes[2 * ch + c]
+            cols = slice(n2 * 512, n2 * 512 + 512)
+            rows = slice(m * P, m * P + P)
+            nc.tensor.matmul_mx(
+                out=acc[:],
+                lhsT=gc[:, c, rows].bitcast(E5X4),
+                lhsT_scale=gs[:, c, rows],
+                rhs=tck[:, cols].bitcast(E4X4),
+                rhs_scale=tsk[:, cols],
+                start=(c == 0),
+                stop=(c == 1),
+            )
+
+        def leave(acc, ch, n2, m, on_vector):
+            o = opool.tile([P, 512], F32, name="o", tag="o")
+            if on_vector:
+                nc.vector.tensor_scalar_mul(out=o[:], in0=acc[:], scalar1=0.5)
+            else:
+                nc.scalar.activation(out=o[:], in_=acc[:], func=COPY, scale=0.5)
+            nc.sync.dma_start(
+                out=out[m * P : m * P + P, ch * 1024 + n2 * 512 : ch * 1024 + n2 * 512 + 512],
+                in_=o[:],
+            )
+
+        def mx(ch):
             for n2 in range(2):
-                cols = slice(n2 * 512, n2 * 512 + 512)
                 for m in range(4):
-                    rows = slice(m * P, m * P + P)
                     acc = ps_acc.tile([P, 512], F32, name="acc", tag="acc")
-                    for c in range(2):
-                        tck, tsk = codes[2 * ch + c]
-                        nc.tensor.matmul_mx(
-                            out=acc[:],
-                            lhsT=gc[:, c, rows].bitcast(E5X4),
-                            lhsT_scale=gs[:, c, rows],
-                            rhs=tck[:, cols].bitcast(E4X4),
-                            rhs_scale=tsk[:, cols],
-                            start=(c == 0),
-                            stop=(c == 1),
-                        )
-                    o = opool.tile([P, 512], F32, name="o", tag="o")
-                    if share and m % 2 == 1:
-                        nc.vector.tensor_scalar_mul(out=o[:], in0=acc[:], scalar1=0.5)
-                    else:
-                        nc.scalar.activation(out=o[:], in_=acc[:], func=COPY, scale=0.5)
-                    nc.sync.dma_start(
-                        out=out[rows, ch * 1024 + n2 * 512 : ch * 1024 + n2 * 512 + 512], in_=o[:]
-                    )
+                    mx_pass(acc, ch, n2, m, 0)
+                    mx_pass(acc, ch, n2, m, 1)
+                    leave(acc, ch, n2, m, False)
 
         pe_path(0)
         pe_path(1)
         for c in range(2):
             nc.scalar.copy(out=gg[:, c], in_=g_raw[:, c].rearrange("p j m -> p m j"))
-        for k in range(8):
-            st1(k)
-            if k >= 1:
-                quant(k - 1)
-            if k == 1:
+        whole = ((0, V_I),)
+        for k in range(7):
+            st1(k, HEAD if k == 0 else whole)
+            if k == 2:
                 nc.vector.quantize_mx(
                     out=gc.rearrange("p c m -> p (c m)").bitcast(E5X4),
                     scales=gs.rearrange("p c m -> p (c m)"),
                     in_=gg.rearrange("p c m j -> p (c m j)"),
                 )
+            if k >= 1:
+                new_codes(k - 1)
+                quant(k - 1, 0, 1024)
             if k >= 2 and k % 2 == 0:
-                mx(k // 2 - 1, False)
+                mx(k // 2 - 1)
             st2(k)
             if k + 2 < 8:
                 pe_path(k + 2)
-        quant(7)
-        mx(3, True)
+        st1(7, whole)
+        new_codes(6)
+        quant(6, 0, 1024)
+        accs = {}
+        for n2 in range(2):
+            for m in range(4):
+                if n2 == 0:
+                    acc = ps_acc.tile([P, 512], F32, name="acc", tag="acc")
+                elif m < 2:
+                    acc = ps_xt.tile([P, 512], F32, name="acc_x", tag="xtp")
+                else:
+                    acc = ps_hm.tile([P, 512], F32, name="acc_h", tag="hm")
+                accs[(n2, m)] = acc
+                mx_pass(acc, 3, n2, m, 0)
+        new_codes(7)
+        st2_one(7, 0, 0)
+        st2_one(7, 0, 1)
+        st2_one(7, 1, 0)
+        quant(7, 0, 512)
+        for m in range(4):
+            mx_pass(accs[(0, m)], 3, 0, m, 1)
+            leave(accs[(0, m)], 3, 0, m, False)
+        st2_one(7, 1, 1)
+        quant(7, 512, 768)
+        quant(7, 768, 1024)
+        for m in range(4):
+            mx_pass(accs[(1, m)], 3, 1, m, 1)
+            leave(accs[(1, m)], 3, 1, m, m % 2 == 1)

@@ -19,19 +19,19 @@ SUB = mybir.AluOpType.subtract
 COPY = mybir.ActivationFunctionType.Copy
 
 P = 128
-PE_UNITS = 3
-V_I = 16 - 2 * PE_UNITS
-V_Q = V_I * 32
-HEAD = ((0, 2), (2, 5), (5, V_I))
+SLABS = 8
+PE_UNITS = (3, 3, 3, 3, 3, 3, 3, 4)
+HEAD = ((0, 2), (2, 5), (5, 10))
 
 
 def tile_waveletlinearlayer_kernel(tc, x, W, b, grad_out, out):
     nc = tc.nc
     xv = x.rearrange("(c p j) f -> c p j f", c=2, p=P, j=4)
     gv = grad_out.rearrange("(c p j) m -> p c j m", c=2, p=P, j=4)
+    v_i = [16 - 2 * u for u in PE_UNITS]
     with ExitStack() as ctx:
         const = ctx.enter_context(tc.tile_pool(name="const", bufs=1))
-        xpool = ctx.enter_context(tc.tile_pool(name="xpool", bufs=8))
+        xpool = ctx.enter_context(tc.tile_pool(name="xpool", bufs=SLABS))
         spool = ctx.enter_context(tc.tile_pool(name="spool", bufs=2))
         gpool = ctx.enter_context(tc.tile_pool(name="gpool", bufs=3))
         tpool = ctx.enter_context(tc.tile_pool(name="tpool", bufs=4))
@@ -44,7 +44,7 @@ def tile_waveletlinearlayer_kernel(tc, x, W, b, grad_out, out):
             ctx.enter_context(tc.manual_schedule())
 
         xs = []
-        for k in range(8):
+        for k in range(SLABS):
             xk = xpool.tile([P, 4, 512, 2], BF16, name="xk", tag="xk")
             xs.append(xk)
         g_raw = const.tile([P, 2, 4, 512], BF16, name="g_raw")
@@ -59,10 +59,10 @@ def tile_waveletlinearlayer_kernel(tc, x, W, b, grad_out, out):
 
         for i0, i1 in HEAD:
             load_x(0, 64 * i0, 64 * i1)
-        load_x(0, 2 * V_Q, 1024)
+        load_x(0, 64 * v_i[0], 1024)
         load_x(1, 0, 1024)
         nc.sync.dma_start(out=g_raw[:], in_=gv)
-        for k in range(2, 8):
+        for k in range(2, SLABS):
             load_x(k, 0, 1024)
 
         ident = const.tile([P, P], BF16, name="ident")
@@ -79,7 +79,10 @@ def tile_waveletlinearlayer_kernel(tc, x, W, b, grad_out, out):
             )
         for s2, op in ((0, ADD), (1, SUB)):
             nc.vector.tensor_tensor(
-                out=hmat[:, :, s2], in0=hs[:, :, :, 0, :], in1=hs[:, :, :, 1, :], op=op
+                out=hmat[:, s2].rearrange("p i a c -> p a i c"),
+                in0=hs[:, :, :, 0, :],
+                in1=hs[:, :, :, 1, :],
+                op=op,
             )
         hflat = hmat.rearrange("p a b c d -> p (a b c d)")
 
@@ -89,10 +92,11 @@ def tile_waveletlinearlayer_kernel(tc, x, W, b, grad_out, out):
 
         grouped = {}
         codes = {}
+        stage1 = {}
 
         def pe_transposes(k, u):
             xtp = ps_xt.tile([P, 4, P], BF16, name="xtp", tag="xtp")
-            q0 = V_Q + 64 * u
+            q0 = 32 * v_i[k] + 64 * u
             for j in range(4):
                 nc.tensor.transpose(
                     xtp[:, j, :],
@@ -107,53 +111,47 @@ def tile_waveletlinearlayer_kernel(tc, x, W, b, grad_out, out):
             hm = ps_hm.tile([P, 4, P], F32, name="hm", tag="hm")
             for j in range(4):
                 nc.tensor.matmul(hm[:, j, :], lhsT=xt[:, j, :], rhs=hflat, start=True, stop=True)
-            w0 = (V_I + 2 * u) * 64
+            i0 = v_i[k] + 2 * u
             nc.scalar.copy(
-                out=grouped[k]
-                .rearrange("p a b i w -> p (a b) (i w)")[:, :, w0 : w0 + 128]
-                .rearrange("p s (w j) -> p s w j", j=4),
-                in_=hm.rearrange("p j (s w) -> p s w j", s=4),
+                out=grouped[k][:, :, i0 : i0 + 2].rearrange("p s i a (w j) -> p s (i a w) j", j=4),
+                in_=hm.rearrange("p j (s w) -> p s w j", s=2),
             )
 
         def pe_path(k):
-            gk = gpool.tile([P, 2, 2, 16, 64], BF16, name="gk", tag="gk", align_bytes=64)
+            gk = gpool.tile([P, 2, 16, 2, 64], BF16, name="gk", tag="gk", align_bytes=64)
             grouped[k] = gk
-            xt0 = pe_transposes(k, 0)
-            xt1 = pe_transposes(k, 1)
-            pe_matmuls(k, 0, xt0)
-            xt2 = pe_transposes(k, 2)
-            pe_matmuls(k, 1, xt1)
-            pe_matmuls(k, 2, xt2)
-
-        stage1 = {}
+            xts = {}
+            for u in range(PE_UNITS[k] + 1):
+                if u < PE_UNITS[k]:
+                    xts[u] = pe_transposes(k, u)
+                if u >= 1:
+                    pe_matmuls(k, u - 1, xts[u - 1])
 
         def st1(k, pieces):
-            sk = spool.tile([P, 2, V_I, 2, 64], F32, name="sk", tag="sk")
+            sk = spool.tile([P, 16 - 2 * min(PE_UNITS), 2, 2, 64], F32, name="sk", tag="sk")
             stage1[k] = sk
             for i0, i1 in pieces:
                 for pl, op in ((0, ADD), (1, SUB)):
                     nc.vector.tensor_tensor(
-                        out=sk[:, pl, i0:i1].rearrange("p i r (c j e) -> p (i r c) j e", j=4, e=4),
-                        in0=xs[k][:, :, 32 * i0 : 32 * i1, 0].rearrange("p j (c e) -> p c j e", e=4),
-                        in1=xs[k][:, :, 32 * i0 : 32 * i1, 1].rearrange("p j (c e) -> p c j e", e=4),
+                        out=sk[:, i0:i1, pl].rearrange("p i r (c j e) -> p i (r c) j e", c=4, j=4, e=4),
+                        in0=xs[k][:, :, 32 * i0 : 32 * i1, 0].rearrange(
+                            "p j (i c e) -> p i c j e", c=8, e=4
+                        ),
+                        in1=xs[k][:, :, 32 * i0 : 32 * i1, 1].rearrange(
+                            "p j (i c e) -> p i c j e", c=8, e=4
+                        ),
                         op=op,
                     )
 
-        def st2_one(k, pl, s2):
+        def st2(k, s2):
             sk = stage1[k]
+            n = v_i[k]
             nc.vector.tensor_tensor(
-                out=grouped[k][:, pl, s2, 0:V_I, :].rearrange(
-                    "p i (c e j) -> p i c j e", c=4, e=4, j=4
-                ),
-                in0=sk[:, pl, :, 0, :].rearrange("p i (c j e) -> p i c j e", c=4, j=4, e=4),
-                in1=sk[:, pl, :, 1, :].rearrange("p i (c j e) -> p i c j e", c=4, j=4, e=4),
+                out=grouped[k][:, s2, 0:n].rearrange("p i a (c e j) -> p (i a) c j e", c=4, e=4, j=4),
+                in0=sk[:, 0:n, :, 0, :].rearrange("p i a (c j e) -> p (i a) c j e", c=4, j=4, e=4),
+                in1=sk[:, 0:n, :, 1, :].rearrange("p i a (c j e) -> p (i a) c j e", c=4, j=4, e=4),
                 op=(ADD, SUB)[s2],
             )
-
-        def st2(k):
-            for pl in range(2):
-                for s2 in range(2):
-                    st2_one(k, pl, s2)
 
         def new_codes(k):
             tck = tpool.tile([P, 1024], U32, name="tck", tag="tck", align_bytes=64)
@@ -165,12 +163,12 @@ def tile_waveletlinearlayer_kernel(tc, x, W, b, grad_out, out):
             nc.vector.quantize_mx(
                 out=tck[:, w0:w1].bitcast(E4X4),
                 scales=tsk[:, w0:w1],
-                in_=grouped[k].rearrange("p a b i w -> p (a b i w)")[:, 4 * w0 : 4 * w1],
+                in_=grouped[k].rearrange("p s i a w -> p (s i a w)")[:, 4 * w0 : 4 * w1],
             )
 
-        def mx_pass(acc, ch, n2, m, c):
+        def mx_pass(acc, ch, s2, m, c):
             tck, tsk = codes[2 * ch + c]
-            cols = slice(n2 * 512, n2 * 512 + 512)
+            cols = slice(s2 * 512, s2 * 512 + 512)
             rows = slice(m * P, m * P + P)
             nc.tensor.matmul_mx(
                 out=acc[:],
@@ -182,32 +180,38 @@ def tile_waveletlinearlayer_kernel(tc, x, W, b, grad_out, out):
                 stop=(c == 1),
             )
 
-        def leave(acc, ch, n2, m, on_vector):
-            o = opool.tile([P, 512], F32, name="o", tag="o")
+        def leave(acc, ch, s2, m, on_vector):
+            o = opool.tile([P, 2, 16, 16], F32, name="o", tag="o")
+            src = acc.rearrange("p (i a c) -> p a i c", a=2, c=16)
             if on_vector:
-                nc.vector.tensor_scalar_mul(out=o[:], in0=acc[:], scalar1=0.5)
+                nc.vector.tensor_scalar_mul(out=o[:], in0=src, scalar1=0.5)
             else:
-                nc.scalar.activation(out=o[:], in_=acc[:], func=COPY, scale=0.5)
+                nc.scalar.activation(out=o[:], in_=src, func=COPY, scale=0.5)
             nc.sync.dma_start(
-                out=out[m * P : m * P + P, ch * 1024 + n2 * 512 : ch * 1024 + n2 * 512 + 512],
-                in_=o[:],
+                out=out[m * P : m * P + P, ch * 1024 : ch * 1024 + 1024].rearrange(
+                    "p (a s w) -> p a s w", a=2, s=2
+                )[:, :, s2, :],
+                in_=o.rearrange("p a i c -> p a (i c)"),
             )
 
         def mx(ch):
-            for n2 in range(2):
+            for s2 in range(2):
                 for m in range(4):
                     acc = ps_acc.tile([P, 512], F32, name="acc", tag="acc")
-                    mx_pass(acc, ch, n2, m, 0)
-                    mx_pass(acc, ch, n2, m, 1)
-                    leave(acc, ch, n2, m, False)
+                    mx_pass(acc, ch, s2, m, 0)
+                    mx_pass(acc, ch, s2, m, 1)
+                    leave(acc, ch, s2, m, False)
 
         pe_path(0)
         pe_path(1)
         for c in range(2):
-            nc.scalar.copy(out=gg[:, c], in_=g_raw[:, c].rearrange("p j m -> p m j"))
-        whole = ((0, V_I),)
-        for k in range(7):
-            st1(k, HEAD if k == 0 else whole)
+            nc.scalar.copy(
+                out=gg[:, c].rearrange("p (a e) j -> p a j e", e=4),
+                in_=g_raw[:, c].rearrange("p j (a e) -> p a j e", e=4),
+            )
+        last = SLABS - 1
+        for k in range(last):
+            st1(k, HEAD if k == 0 else ((0, v_i[k]),))
             if k == 2:
                 nc.vector.quantize_mx(
                     out=gc.rearrange("p c m -> p (c m)").bitcast(E5X4),
@@ -219,34 +223,34 @@ def tile_waveletlinearlayer_kernel(tc, x, W, b, grad_out, out):
                 quant(k - 1, 0, 1024)
             if k >= 2 and k % 2 == 0:
                 mx(k // 2 - 1)
-            st2(k)
-            if k + 2 < 8:
+            st2(k, 0)
+            st2(k, 1)
+            if k + 2 < SLABS:
                 pe_path(k + 2)
-        st1(7, whole)
-        new_codes(6)
-        quant(6, 0, 1024)
+        assert v_i[last] == 8
+        st1(last, ((0, v_i[last]),))
+        new_codes(last - 1)
+        quant(last - 1, 0, 1024)
         accs = {}
-        for n2 in range(2):
+        for s2 in range(2):
             for m in range(4):
-                if n2 == 0:
+                if s2 == 0:
                     acc = ps_acc.tile([P, 512], F32, name="acc", tag="acc")
                 elif m < 2:
                     acc = ps_xt.tile([P, 512], F32, name="acc_x", tag="xtp")
                 else:
                     acc = ps_hm.tile([P, 512], F32, name="acc_h", tag="hm")
-                accs[(n2, m)] = acc
-                mx_pass(acc, 3, n2, m, 0)
-        new_codes(7)
-        st2_one(7, 0, 0)
-        st2_one(7, 0, 1)
-        st2_one(7, 1, 0)
-        quant(7, 0, 512)
+                accs[(s2, m)] = acc
+                mx_pass(acc, 3, s2, m, 0)
+        new_codes(last)
+        st2(last, 0)
+        quant(last, 768, 1024)
+        quant(last, 0, 512)
         for m in range(4):
             mx_pass(accs[(0, m)], 3, 0, m, 1)
             leave(accs[(0, m)], 3, 0, m, False)
-        st2_one(7, 1, 1)
-        quant(7, 512, 768)
-        quant(7, 768, 1024)
+        st2(last, 1)
+        quant(last, 512, 768)
         for m in range(4):
             mx_pass(accs[(1, m)], 3, 1, m, 1)
             leave(accs[(1, m)], 3, 1, m, m % 2 == 1)

@@ -33,7 +33,7 @@ def tile_waveletlinearlayer_kernel(tc, x, W, b, grad_out, out):
         const = ctx.enter_context(tc.tile_pool(name="const", bufs=1))
         xpool = ctx.enter_context(tc.tile_pool(name="xpool", bufs=SLABS))
         spool = ctx.enter_context(tc.tile_pool(name="spool", bufs=2))
-        gpool = ctx.enter_context(tc.tile_pool(name="gpool", bufs=3))
+        gpool = ctx.enter_context(tc.tile_pool(name="gpool", bufs=4))
         tpool = ctx.enter_context(tc.tile_pool(name="tpool", bufs=4))
         xtpool = ctx.enter_context(tc.tile_pool(name="xtpool", bufs=3))
         opool = ctx.enter_context(tc.tile_pool(name="opool", bufs=8))
@@ -194,13 +194,12 @@ def tile_waveletlinearlayer_kernel(tc, x, W, b, grad_out, out):
                 in_=o.rearrange("p a i c -> p a (i c)"),
             )
 
-        def mx(ch):
-            for s2 in range(2):
-                for m in range(4):
-                    acc = ps_acc.tile([P, 512], F32, name="acc", tag="acc")
-                    mx_pass(acc, ch, s2, m, 0)
-                    mx_pass(acc, ch, s2, m, 1)
-                    leave(acc, ch, s2, m, False)
+        def mx(ch, s2):
+            for m in range(4):
+                acc = ps_acc.tile([P, 512], F32, name="acc", tag="acc")
+                mx_pass(acc, ch, s2, m, 0)
+                mx_pass(acc, ch, s2, m, 1)
+                leave(acc, ch, s2, m, False)
 
         pe_path(0)
         pe_path(1)
@@ -209,48 +208,55 @@ def tile_waveletlinearlayer_kernel(tc, x, W, b, grad_out, out):
                 out=gg[:, c].rearrange("p (a e) j -> p a j e", e=4),
                 in_=g_raw[:, c].rearrange("p j (a e) -> p a j e", e=4),
             )
-        last = SLABS - 1
-        for k in range(last):
-            st1(k, HEAD if k == 0 else ((0, v_i[k]),))
-            if k == 2:
+        for ch in range(4):
+            k0 = 2 * ch
+            k1 = k0 + 1
+            st1(k0, HEAD if ch == 0 else ((0, v_i[k0]),))
+            if ch == 1:
                 nc.vector.quantize_mx(
                     out=gc.rearrange("p c m -> p (c m)").bitcast(E5X4),
                     scales=gs.rearrange("p c m -> p (c m)"),
                     in_=gg.rearrange("p c m j -> p (c m j)"),
                 )
-            if k >= 1:
-                new_codes(k - 1)
-                quant(k - 1, 0, 1024)
-            if k >= 2 and k % 2 == 0:
-                mx(k // 2 - 1)
-            st2(k, 0)
-            st2(k, 1)
-            if k + 2 < SLABS:
-                pe_path(k + 2)
-        assert v_i[last] == 8
-        st1(last, ((0, v_i[last]),))
-        new_codes(last - 1)
-        quant(last - 1, 0, 1024)
-        accs = {}
-        for s2 in range(2):
-            for m in range(4):
-                if s2 == 0:
-                    acc = ps_acc.tile([P, 512], F32, name="acc", tag="acc")
-                elif m < 2:
-                    acc = ps_xt.tile([P, 512], F32, name="acc_x", tag="xtp")
-                else:
-                    acc = ps_hm.tile([P, 512], F32, name="acc_h", tag="hm")
-                accs[(s2, m)] = acc
-                mx_pass(acc, 3, s2, m, 0)
-        new_codes(last)
-        st2(last, 0)
-        quant(last, 768, 1024)
-        quant(last, 0, 512)
+                mx(0, 0)
+                mx(0, 1)
+            st1(k1, ((0, v_i[k1]),))
+            if ch < 3:
+                pe_path(k0 + 2)
+                pe_path(k1 + 2)
+            new_codes(k0)
+            new_codes(k1)
+            st2(k0, 0)
+            st2(k1, 0)
+            if ch == 0:
+                st2(k0, 1)
+                st2(k1, 1)
+                quant(k0, 0, 1024)
+                quant(k1, 0, 1024)
+                continue
+            quant(k0, 0, 512)
+            quant(k1, 0, 512)
+            mx(ch, 0)
+            if ch < 3:
+                st2(k0, 1)
+                st2(k1, 1)
+                quant(k0, 512, 1024)
+                quant(k1, 512, 1024)
+                mx(ch, 1)
+        assert v_i[7] == 8
+        st2(6, 1)
+        quant(7, 768, 1024)
+        st2(7, 1)
+        quant(6, 512, 1024)
+        accs = []
         for m in range(4):
-            mx_pass(accs[(0, m)], 3, 0, m, 1)
-            leave(accs[(0, m)], 3, 0, m, False)
-        st2(last, 1)
-        quant(last, 512, 768)
+            if m < 2:
+                acc = ps_xt.tile([P, 512], F32, name="acc_x", tag="xtp")
+            else:
+                acc = ps_hm.tile([P, 512], F32, name="acc_h", tag="hm")
+            accs.append(acc)
+            mx_pass(acc, 3, 1, m, 0)
+        quant(7, 512, 768)
         for m in range(4):
-            mx_pass(accs[(1, m)], 3, 1, m, 1)
-            leave(accs[(1, m)], 3, 1, m, m % 2 == 1)
+            mx_pass(accs[m], 3, 1, m, 1)
+            leave(accs[m], 3, 1, m, m % 2 == 1)

@@ -31,7 +31,7 @@ def tile_waveletlinearlayer_kernel(tc, x, W, b, grad_out, out):
     v_i = [16 - 2 * u for u in PE_UNITS]
     with ExitStack() as ctx:
         const = ctx.enter_context(tc.tile_pool(name="const", bufs=1))
-        xpool = ctx.enter_context(tc.tile_pool(name="xpool", bufs=SLABS))
+        xpool = ctx.enter_context(tc.tile_pool(name="xpool", bufs=1))
         spool = ctx.enter_context(tc.tile_pool(name="spool", bufs=2))
         gpool = ctx.enter_context(tc.tile_pool(name="gpool", bufs=4))
         tpool = ctx.enter_context(tc.tile_pool(name="tpool", bufs=4))
@@ -43,27 +43,34 @@ def tile_waveletlinearlayer_kernel(tc, x, W, b, grad_out, out):
         if MANUAL:
             ctx.enter_context(tc.manual_schedule())
 
-        xs = []
-        for k in range(SLABS):
-            xk = xpool.tile([P, 4, 512, 2], BF16, name="xk", tag="xk")
-            xs.append(xk)
+        x_tiles = {}
         g_raw = const.tile([P, 2, 4, 512], BF16, name="g_raw")
 
-        def load_x(k, f0, f1):
-            c = k % 2
-            ch = k // 2
+        def load_x(k, i0, i1):
+            xk = xpool.tile(
+                [P, 4, 32 * (i1 - i0), 2], BF16, name="x%d_%d" % (k, i0), tag="x%d_%d" % (k, i0)
+            )
+            x_tiles[k] = x_tiles.get(k, []) + [(i0, i1, xk)]
+            f0 = (k // 2) * 1024 + 64 * i0
             nc.sync.dma_start(
-                out=xs[k].rearrange("p j q e -> p j (q e)")[:, :, f0:f1],
-                in_=xv[c][:, :, ch * 1024 + f0 : ch * 1024 + f1],
+                out=xk.rearrange("p j q e -> p j (q e)"),
+                in_=xv[k % 2][:, :, f0 : f0 + 64 * (i1 - i0)],
             )
 
+        def x_rows(k, i0, i1):
+            for s0, s1, xk in x_tiles[k]:
+                if s0 <= i0 and i1 <= s1:
+                    return xk[:, :, 32 * (i0 - s0) : 32 * (i1 - s0), :]
+            raise ValueError("rows %d to %d of slab %d lie in no one tile" % (i0, i1, k))
+
         for i0, i1 in HEAD:
-            load_x(0, 64 * i0, 64 * i1)
-        load_x(0, 64 * v_i[0], 1024)
-        load_x(1, 0, 1024)
+            load_x(0, i0, i1)
+        load_x(0, v_i[0], 16)
+        load_x(1, 0, v_i[1])
+        load_x(1, v_i[1], 16)
         nc.sync.dma_start(out=g_raw[:], in_=gv)
         for k in range(2, SLABS):
-            load_x(k, 0, 1024)
+            load_x(k, 0, 16)
 
         ident = const.tile([P, P], BF16, name="ident")
         make_identity(nc, ident[:])
@@ -96,12 +103,10 @@ def tile_waveletlinearlayer_kernel(tc, x, W, b, grad_out, out):
 
         def pe_transposes(k, u):
             xtp = ps_xt.tile([P, 4, P], BF16, name="xtp", tag="xtp")
-            q0 = 32 * v_i[k] + 64 * u
+            block = x_rows(k, v_i[k] + 2 * u, v_i[k] + 2 * u + 2)
             for j in range(4):
                 nc.tensor.transpose(
-                    xtp[:, j, :],
-                    xs[k][:, j, q0 : q0 + 64, :].rearrange("p q e -> p (q e)"),
-                    ident[:],
+                    xtp[:, j, :], block[:, j].rearrange("p q e -> p (q e)"), ident[:]
                 )
             xt = xtpool.tile([P, 4, P], BF16, name="xt", tag="xt")
             nc.scalar.copy(out=xt[:], in_=xtp[:])
@@ -127,21 +132,18 @@ def tile_waveletlinearlayer_kernel(tc, x, W, b, grad_out, out):
                 if u >= 1:
                     pe_matmuls(k, u - 1, xts[u - 1])
 
-        def st1(k, pieces):
-            sk = spool.tile([P, 16 - 2 * min(PE_UNITS), 2, 2, 64], F32, name="sk", tag="sk")
-            stage1[k] = sk
-            for i0, i1 in pieces:
-                for pl, op in ((0, ADD), (1, SUB)):
-                    nc.vector.tensor_tensor(
-                        out=sk[:, i0:i1, pl].rearrange("p i r (c j e) -> p i (r c) j e", c=4, j=4, e=4),
-                        in0=xs[k][:, :, 32 * i0 : 32 * i1, 0].rearrange(
-                            "p j (i c e) -> p i c j e", c=8, e=4
-                        ),
-                        in1=xs[k][:, :, 32 * i0 : 32 * i1, 1].rearrange(
-                            "p j (i c e) -> p i c j e", c=8, e=4
-                        ),
-                        op=op,
-                    )
+        def st1_plane(k, pl, i0, i1):
+            if k not in stage1:
+                sk = spool.tile([P, 16 - 2 * min(PE_UNITS), 2, 2, 64], F32, name="sk", tag="sk")
+                stage1[k] = sk
+            nc.vector.tensor_tensor(
+                out=stage1[k][:, i0:i1, pl].rearrange(
+                    "p i r (c j e) -> p i (r c) j e", c=4, j=4, e=4
+                ),
+                in0=x_rows(k, i0, i1)[:, :, :, 0].rearrange("p j (i c e) -> p i c j e", c=8, e=4),
+                in1=x_rows(k, i0, i1)[:, :, :, 1].rearrange("p j (i c e) -> p i c j e", c=8, e=4),
+                op=(ADD, SUB)[pl],
+            )
 
         def st2(k, s2):
             sk = stage1[k]
@@ -208,55 +210,88 @@ def tile_waveletlinearlayer_kernel(tc, x, W, b, grad_out, out):
                 out=gg[:, c].rearrange("p (a e) j -> p a j e", e=4),
                 in_=g_raw[:, c].rearrange("p j (a e) -> p a j e", e=4),
             )
-        for ch in range(4):
+        def quant_g():
+            nc.vector.quantize_mx(
+                out=gc.rearrange("p c m -> p (c m)").bitcast(E5X4),
+                scales=gs.rearrange("p c m -> p (c m)"),
+                in_=gg.rearrange("p c m j -> p (c m j)"),
+            )
+
+        h0, h1, h2 = HEAD
+        st1_plane(0, 0, h0[0], h0[1])
+        st1_plane(0, 0, h1[0], h1[1])
+        st1_plane(0, 1, h0[0], h0[1])
+        st1_plane(0, 1, h1[0], h1[1])
+        st1_plane(0, 0, h2[0], h2[1])
+        st1_plane(0, 1, h2[0], h2[1])
+        st1_plane(1, 0, 0, v_i[1])
+        st2(0, 0)
+        st1_plane(1, 1, 0, v_i[1])
+        st2(0, 1)
+        pe_path(2)
+        pe_path(3)
+        st2(1, 0)
+        st2(1, 1)
+        new_codes(0)
+        new_codes(1)
+        quant(0, 0, 1024)
+        quant(1, 0, 1024)
+        for ch in (1, 2):
             k0 = 2 * ch
             k1 = k0 + 1
-            st1(k0, HEAD if ch == 0 else ((0, v_i[k0]),))
+            st1_plane(k0, 0, 0, v_i[k0])
             if ch == 1:
-                nc.vector.quantize_mx(
-                    out=gc.rearrange("p c m -> p (c m)").bitcast(E5X4),
-                    scales=gs.rearrange("p c m -> p (c m)"),
-                    in_=gg.rearrange("p c m j -> p (c m j)"),
-                )
+                quant_g()
                 mx(0, 0)
                 mx(0, 1)
-            st1(k1, ((0, v_i[k1]),))
-            if ch < 3:
-                pe_path(k0 + 2)
-                pe_path(k1 + 2)
+            st1_plane(k1, 0, 0, v_i[k1])
+            st1_plane(k0, 1, 0, v_i[k0])
+            st1_plane(k1, 1, 0, v_i[k1])
+            pe_path(k0 + 2)
+            pe_path(k1 + 2)
             new_codes(k0)
             new_codes(k1)
-            st2(k0, 0)
-            st2(k1, 0)
-            if ch == 0:
-                st2(k0, 1)
-                st2(k1, 1)
-                quant(k0, 0, 1024)
-                quant(k1, 0, 1024)
-                continue
-            quant(k0, 0, 512)
-            quant(k1, 0, 512)
-            mx(ch, 0)
-            if ch < 3:
-                st2(k0, 1)
-                st2(k1, 1)
-                quant(k0, 512, 1024)
-                quant(k1, 512, 1024)
-                mx(ch, 1)
+            for s2 in range(2):
+                st2(k0, s2)
+                st2(k1, s2)
+                quant(k0, 512 * s2, 512 * s2 + 512)
+                quant(k1, 512 * s2, 512 * s2 + 512)
+                mx(ch, s2)
         assert v_i[7] == 8
+        accs = {}
+
+        def open_groups(s2):
+            for m in range(4):
+                if s2 == 0:
+                    acc = ps_acc.tile([P, 512], F32, name="acc", tag="acc")
+                elif m < 2:
+                    acc = ps_xt.tile([P, 512], F32, name="acc_x", tag="xtp")
+                else:
+                    acc = ps_hm.tile([P, 512], F32, name="acc_h", tag="hm")
+                accs[(s2, m)] = acc
+                mx_pass(acc, 3, s2, m, 0)
+
+        def close_groups(s2, share):
+            for m in range(4):
+                mx_pass(accs[(s2, m)], 3, s2, m, 1)
+                leave(accs[(s2, m)], 3, s2, m, share and m % 2 == 1)
+
+        new_codes(6)
+        new_codes(7)
+        st1_plane(6, 0, 0, v_i[6])
+        st1_plane(7, 0, 0, v_i[7])
+        st1_plane(6, 1, 0, v_i[6])
+        st1_plane(7, 1, 0, v_i[7])
+        st2(6, 0)
+        st2(7, 0)
+        quant(6, 0, 512)
+        open_groups(0)
         st2(6, 1)
-        quant(7, 768, 1024)
-        st2(7, 1)
+        quant(7, 0, 512)
+        close_groups(0, False)
         quant(6, 512, 1024)
-        accs = []
-        for m in range(4):
-            if m < 2:
-                acc = ps_xt.tile([P, 512], F32, name="acc_x", tag="xtp")
-            else:
-                acc = ps_hm.tile([P, 512], F32, name="acc_h", tag="hm")
-            accs.append(acc)
-            mx_pass(acc, 3, 1, m, 0)
+        open_groups(1)
+        st2(7, 1)
+        quant(7, 768, 1024)
         quant(7, 512, 768)
-        for m in range(4):
-            mx_pass(accs[m], 3, 1, m, 1)
-            leave(accs[m], 3, 1, m, m % 2 == 1)
+        close_groups(1, True)

@@ -65,8 +65,8 @@ def tile_waveletlinearlayer_kernel(tc, x, W, b, grad_out, out):
 
         for i0, i1 in HEAD:
             load_x(0, i0, i1)
-        load_x(0, v_i[0], 16)
         load_x(1, 0, v_i[1])
+        load_x(0, v_i[0], 16)
         load_x(1, v_i[1], 16)
         nc.sync.dma_start(out=g_raw[:], in_=gv)
         for k in range(2, SLABS):
@@ -240,11 +240,11 @@ def tile_waveletlinearlayer_kernel(tc, x, W, b, grad_out, out):
             k0 = 2 * ch
             k1 = k0 + 1
             st1_plane(k0, 0, 0, v_i[k0])
+            st1_plane(k1, 0, 0, v_i[k1])
             if ch == 1:
                 quant_g()
                 mx(0, 0)
                 mx(0, 1)
-            st1_plane(k1, 0, 0, v_i[k1])
             st1_plane(k0, 1, 0, v_i[k0])
             st1_plane(k1, 1, 0, v_i[k1])
             pe_path(k0 + 2)

@@ -138,10 +138,10 @@ def tile_waveletlinearlayer_kernel(tc, x, W, b, grad_out, out):
                 stage1[k] = sk
             nc.vector.tensor_tensor(
                 out=stage1[k][:, i0:i1, pl].rearrange(
-                    "p i r (c j e) -> p i (r c) j e", c=4, j=4, e=4
+                    "p i r (c j e) -> p i (r c) j e", c=2, j=4, e=8
                 ),
-                in0=x_rows(k, i0, i1)[:, :, :, 0].rearrange("p j (i c e) -> p i c j e", c=8, e=4),
-                in1=x_rows(k, i0, i1)[:, :, :, 1].rearrange("p j (i c e) -> p i c j e", c=8, e=4),
+                in0=x_rows(k, i0, i1)[:, :, :, 0].rearrange("p j (i c e) -> p i c j e", c=4, e=8),
+                in1=x_rows(k, i0, i1)[:, :, :, 1].rearrange("p j (i c e) -> p i c j e", c=4, e=8),
                 op=(ADD, SUB)[pl],
             )
 
@@ -149,9 +149,9 @@ def tile_waveletlinearlayer_kernel(tc, x, W, b, grad_out, out):
             sk = stage1[k]
             n = v_i[k]
             nc.vector.tensor_tensor(
-                out=grouped[k][:, s2, 0:n].rearrange("p i a (c e j) -> p (i a) c j e", c=4, e=4, j=4),
-                in0=sk[:, 0:n, :, 0, :].rearrange("p i a (c j e) -> p (i a) c j e", c=4, j=4, e=4),
-                in1=sk[:, 0:n, :, 1, :].rearrange("p i a (c j e) -> p (i a) c j e", c=4, j=4, e=4),
+                out=grouped[k][:, s2, 0:n].rearrange("p i a (c e j) -> p (i a) c j e", c=2, e=8, j=4),
+                in0=sk[:, 0:n, :, 0, :].rearrange("p i a (c j e) -> p (i a) c j e", c=2, j=4, e=8),
+                in1=sk[:, 0:n, :, 1, :].rearrange("p i a (c j e) -> p (i a) c j e", c=2, j=4, e=8),
                 op=(ADD, SUB)[s2],
             )
 

@@ -35,7 +35,7 @@ def tile_waveletlinearlayer_kernel(tc, x, W, b, grad_out, out):
         spool = ctx.enter_context(tc.tile_pool(name="spool", bufs=2))
         gpool = ctx.enter_context(tc.tile_pool(name="gpool", bufs=4))
         tpool = ctx.enter_context(tc.tile_pool(name="tpool", bufs=4))
-        xtpool = ctx.enter_context(tc.tile_pool(name="xtpool", bufs=3))
+        xtpool = ctx.enter_context(tc.tile_pool(name="xtpool", bufs=4))
         opool = ctx.enter_context(tc.tile_pool(name="opool", bufs=8))
         ps_xt = ctx.enter_context(tc.psum_pool(name="ps_xt", bufs=2))
         ps_hm = ctx.enter_context(tc.psum_pool(name="ps_hm", bufs=2))
@@ -112,25 +112,33 @@ def tile_waveletlinearlayer_kernel(tc, x, W, b, grad_out, out):
             nc.scalar.copy(out=xt[:], in_=xtp[:])
             return xt
 
-        def pe_matmuls(k, u, xt):
-            hm = ps_hm.tile([P, 4, P], F32, name="hm", tag="hm")
-            for j in range(4):
-                nc.tensor.matmul(hm[:, j, :], lhsT=xt[:, j, :], rhs=hflat, start=True, stop=True)
-            i0 = v_i[k] + 2 * u
+        def pe_matmuls(k, units, xt_of):
+            n = len(units)
+            hm = ps_hm.tile([P, n, 4, P], BF16, name="hm", tag="hm")
+            for t, u in enumerate(units):
+                for j in range(4):
+                    nc.tensor.matmul(
+                        hm[:, t, j, :], lhsT=xt_of[u][:, j, :], rhs=hflat, start=True, stop=True
+                    )
+            i0 = v_i[k] + 2 * units[0]
             nc.scalar.copy(
-                out=grouped[k][:, :, i0 : i0 + 2].rearrange("p s i a (w j) -> p s (i a w) j", j=4),
-                in_=hm.rearrange("p j (s w) -> p s w j", s=2),
+                out=grouped[k][:, :, i0 : i0 + 2 * n].rearrange(
+                    "p s (t i) a (w j) -> p s t (i a w) j", t=n, j=4
+                ),
+                in_=hm.rearrange("p t j (s w) -> p s t w j", s=2),
             )
 
         def pe_path(k):
             gk = gpool.tile([P, 2, 16, 2, 64], BF16, name="gk", tag="gk", align_bytes=64)
             grouped[k] = gk
             xts = {}
-            for u in range(PE_UNITS[k] + 1):
-                if u < PE_UNITS[k]:
-                    xts[u] = pe_transposes(k, u)
-                if u >= 1:
-                    pe_matmuls(k, u - 1, xts[u - 1])
+            pairs = [tuple(range(u, min(u + 2, PE_UNITS[k]))) for u in range(0, PE_UNITS[k], 2)]
+            for n in range(len(pairs) + 1):
+                if n < len(pairs):
+                    for u in pairs[n]:
+                        xts[u] = pe_transposes(k, u)
+                if n >= 1:
+                    pe_matmuls(k, pairs[n - 1], xts)
 
         def st1_plane(k, pl, i0, i1):
             if k not in stage1:
@@ -262,7 +270,7 @@ def tile_waveletlinearlayer_kernel(tc, x, W, b, grad_out, out):
 
         def open_groups(s2):
             for m in range(4):
-                if s2 == 0:
+                if s2 == 1:
                     acc = ps_acc.tile([P, 512], F32, name="acc", tag="acc")
                 elif m < 2:
                     acc = ps_xt.tile([P, 512], F32, name="acc_x", tag="xtp")

@@ -21,7 +21,7 @@ COPY = mybir.ActivationFunctionType.Copy
 P = 128
 SLABS = 8
 PE_UNITS = (3, 3, 3, 3, 3, 3, 3, 4)
-HEAD = ((0, 2), (2, 5), (5, 10))
+HEAD = ((0, 4), (4, 10))
 
 
 def tile_waveletlinearlayer_kernel(tc, x, W, b, grad_out, out):
@@ -225,13 +225,9 @@ def tile_waveletlinearlayer_kernel(tc, x, W, b, grad_out, out):
                 in_=gg.rearrange("p c m j -> p (c m j)"),
             )
 
-        h0, h1, h2 = HEAD
-        st1_plane(0, 0, h0[0], h0[1])
-        st1_plane(0, 0, h1[0], h1[1])
-        st1_plane(0, 1, h0[0], h0[1])
-        st1_plane(0, 1, h1[0], h1[1])
-        st1_plane(0, 0, h2[0], h2[1])
-        st1_plane(0, 1, h2[0], h2[1])
+        for i0, i1 in HEAD:
+            st1_plane(0, 0, i0, i1)
+            st1_plane(0, 1, i0, i1)
         st1_plane(1, 0, 0, v_i[1])
         st2(0, 0)
         st1_plane(1, 1, 0, v_i[1])

@@ -290,12 +290,12 @@ def tile_waveletlinearlayer_kernel(tc, x, W, b, grad_out, out):
         st2(7, 0)
         quant(6, 0, 512)
         open_groups(0)
-        st2(6, 1)
         quant(7, 0, 512)
         close_groups(0, False)
+        st2(6, 1)
+        st2(7, 1)
         quant(6, 512, 1024)
         open_groups(1)
-        st2(7, 1)
         quant(7, 768, 1024)
         quant(7, 512, 768)
         close_groups(1, True)

from contextlib import ExitStack

import concourse.mybir as mybir
from concourse.masks import make_identity

FLOPS = 2 * 512 * 1024 * 4096
BYTES = 1024 * 4096 * 2 + 1024 * 512 * 2 + 512 * 4096 * 4

MANUAL = True

BF16 = mybir.dt.bfloat16
F32 = mybir.dt.float32
U32 = mybir.dt.uint32
U8 = mybir.dt.uint8
E4X4 = mybir.dt.float8_e4m3fn_x4
E5X4 = mybir.dt.float8_e5m2_x4
ADD = mybir.AluOpType.add
SUB = mybir.AluOpType.subtract
COPY = mybir.ActivationFunctionType.Copy

P = 128
SLABS = 8
PE_UNITS = (3, 3, 3, 3, 3, 3, 3, 4)
HEAD = ((0, 4), (4, 10))


def tile_waveletlinearlayer_kernel(tc, x, W, b, grad_out, out):
    nc = tc.nc
    xv = x.rearrange("(c p j) f -> c p j f", c=2, p=P, j=4)
    gv = grad_out.rearrange("(c p j) m -> p c j m", c=2, p=P, j=4)
    v_i = [16 - 2 * u for u in PE_UNITS]
    with ExitStack() as ctx:
        const = ctx.enter_context(tc.tile_pool(name="const", bufs=1))
        xpool = ctx.enter_context(tc.tile_pool(name="xpool", bufs=1))
        spool = ctx.enter_context(tc.tile_pool(name="spool", bufs=2))
        gpool = ctx.enter_context(tc.tile_pool(name="gpool", bufs=4))
        tpool = ctx.enter_context(tc.tile_pool(name="tpool", bufs=4))
        xtpool = ctx.enter_context(tc.tile_pool(name="xtpool", bufs=4))
        opool = ctx.enter_context(tc.tile_pool(name="opool", bufs=8))
        ps_xt = ctx.enter_context(tc.psum_pool(name="ps_xt", bufs=2))
        ps_hm = ctx.enter_context(tc.psum_pool(name="ps_hm", bufs=2))
        ps_acc = ctx.enter_context(tc.psum_pool(name="ps_acc", bufs=4))
        if MANUAL:
            ctx.enter_context(tc.manual_schedule())

        x_tiles = {}
        g_raw = const.tile([P, 2, 4, 512], BF16, name="g_raw")

        def load_x(k, i0, i1):
            xk = xpool.tile(
                [P, 4, 32 * (i1 - i0), 2], BF16, name="x%d_%d" % (k, i0), tag="x%d_%d" % (k, i0)
            )
            x_tiles[k] = x_tiles.get(k, []) + [(i0, i1, xk)]
            f0 = (k // 2) * 1024 + 64 * i0
            nc.sync.dma_start(
                out=xk.rearrange("p j q e -> p j (q e)"),
                in_=xv[k % 2][:, :, f0 : f0 + 64 * (i1 - i0)],
            )

        def x_rows(k, i0, i1):
            for s0, s1, xk in x_tiles[k]:
                if s0 <= i0 and i1 <= s1:
                    return xk[:, :, 32 * (i0 - s0) : 32 * (i1 - s0), :]
            raise ValueError("rows %d to %d of slab %d lie in no one tile" % (i0, i1, k))

        for i0, i1 in HEAD:
            load_x(0, i0, i1)
        load_x(1, 0, v_i[1])
        load_x(0, v_i[0], 16)
        load_x(1, v_i[1], 16)
        nc.sync.dma_start(out=g_raw[:], in_=gv)
        for k in range(2, SLABS):
            load_x(k, 0, 16)

        ident = const.tile([P, P], BF16, name="ident")
        make_identity(nc, ident[:])
        hs = const.tile([P, 2, 2, 2, 16], BF16, name="hs")
        hmat = const.tile([P, 2, 2, 2, 16], BF16, name="hmat")
        idv = ident.rearrange("p (q e) -> p q e", e=2)
        for pl, op in ((0, ADD), (1, SUB)):
            nc.vector.tensor_tensor(
                out=hs[:, pl].rearrange("p a r c -> p (a r c)"),
                in0=idv[:, :, 0],
                in1=idv[:, :, 1],
                op=op,
            )
        for s2, op in ((0, ADD), (1, SUB)):
            nc.vector.tensor_tensor(
                out=hmat[:, s2].rearrange("p i a c -> p a i c"),
                in0=hs[:, :, :, 0, :],
                in1=hs[:, :, :, 1, :],
                op=op,
            )
        hflat = hmat.rearrange("p a b c d -> p (a b c d)")

        gg = const.tile([P, 2, 512, 4], BF16, name="gg", align_bytes=64)
        gc = const.tile([P, 2, 512], U32, name="gc", align_bytes=64)
        gs = const.tile([P, 2, 512], U8, name="gs", align_bytes=64)

        grouped = {}
        codes = {}
        stage1 = {}

        def pe_transposes(k, u):
            xtp = ps_xt.tile([P, 4, P], BF16, name="xtp", tag="xtp")
            block = x_rows(k, v_i[k] + 2 * u, v_i[k] + 2 * u + 2)
            for j in range(4):
                nc.tensor.transpose(
                    xtp[:, j, :], block[:, j].rearrange("p q e -> p (q e)"), ident[:]
                )
            xt = xtpool.tile([P, 4, P], BF16, name="xt", tag="xt")
            nc.scalar.copy(out=xt[:], in_=xtp[:])
            return xt

        def pe_matmuls(k, units, xt_of):
            n = len(units)
            hm = ps_hm.tile([P, n, 4, P], BF16, name="hm", tag="hm")
            for t, u in enumerate(units):
                for j in range(4):
                    nc.tensor.matmul(
                        hm[:, t, j, :], lhsT=xt_of[u][:, j, :], rhs=hflat, start=True, stop=True
                    )
            i0 = v_i[k] + 2 * units[0]
            nc.scalar.copy(
                out=grouped[k][:, :, i0 : i0 + 2 * n].rearrange(
                    "p s (t i) a (w j) -> p s t (i a w) j", t=n, j=4
                ),
                in_=hm.rearrange("p t j (s w) -> p s t w j", s=2),
            )

        def pe_path(k):
            gk = gpool.tile([P, 2, 16, 2, 64], BF16, name="gk", tag="gk", align_bytes=64)
            grouped[k] = gk
            xts = {}
            pairs = [tuple(range(u, min(u + 2, PE_UNITS[k]))) for u in range(0, PE_UNITS[k], 2)]
            for n in range(len(pairs) + 1):
                if n < len(pairs):
                    for u in pairs[n]:
                        xts[u] = pe_transposes(k, u)
                if n >= 1:
                    pe_matmuls(k, pairs[n - 1], xts)

        def st1_plane(k, pl, i0, i1):
            if k not in stage1:
                sk = spool.tile([P, 16 - 2 * min(PE_UNITS), 2, 2, 64], F32, name="sk", tag="sk")
                stage1[k] = sk
            nc.vector.tensor_tensor(
                out=stage1[k][:, i0:i1, pl].rearrange(
                    "p i r (c j e) -> p i (r c) j e", c=2, j=4, e=8
                ),
                in0=x_rows(k, i0, i1)[:, :, :, 0].rearrange("p j (i c e) -> p i c j e", c=4, e=8),
                in1=x_rows(k, i0, i1)[:, :, :, 1].rearrange("p j (i c e) -> p i c j e", c=4, e=8),
                op=(ADD, SUB)[pl],
            )

        def st2(k, s2):
            sk = stage1[k]
            n = v_i[k]
            nc.vector.tensor_tensor(
                out=grouped[k][:, s2, 0:n].rearrange("p i a (c e j) -> p (i a) c j e", c=2, e=8, j=4),
                in0=sk[:, 0:n, :, 0, :].rearrange("p i a (c j e) -> p (i a) c j e", c=2, j=4, e=8),
                in1=sk[:, 0:n, :, 1, :].rearrange("p i a (c j e) -> p (i a) c j e", c=2, j=4, e=8),
                op=(ADD, SUB)[s2],
            )

        def new_codes(k):
            tck = tpool.tile([P, 1024], U32, name="tck", tag="tck", align_bytes=64)
            tsk = tpool.tile([P, 1024], U8, name="tsk", tag="tsk", align_bytes=64)
            codes[k] = (tck, tsk)

        def quant(k, w0, w1):
            tck, tsk = codes[k]
            nc.vector.quantize_mx(
                out=tck[:, w0:w1].bitcast(E4X4),
                scales=tsk[:, w0:w1],
                in_=grouped[k].rearrange("p s i a w -> p (s i a w)")[:, 4 * w0 : 4 * w1],
            )

        def mx_pass(acc, ch, s2, m, c):
            tck, tsk = codes[2 * ch + c]
            cols = slice(s2 * 512, s2 * 512 + 512)
            rows = slice(m * P, m * P + P)
            nc.tensor.matmul_mx(
                out=acc[:],
                lhsT=gc[:, c, rows].bitcast(E5X4),
                lhsT_scale=gs[:, c, rows],
                rhs=tck[:, cols].bitcast(E4X4),
                rhs_scale=tsk[:, cols],
                start=(c == 0),
                stop=(c == 1),
            )

        def leave(acc, ch, s2, m, on_vector):
            o = opool.tile([P, 2, 16, 16], F32, name="o", tag="o")
            src = acc.rearrange("p (i a c) -> p a i c", a=2, c=16)
            if on_vector:
                nc.vector.tensor_scalar_mul(out=o[:], in0=src, scalar1=0.5)
            else:
                nc.scalar.activation(out=o[:], in_=src, func=COPY, scale=0.5)
            nc.sync.dma_start(
                out=out[m * P : m * P + P, ch * 1024 : ch * 1024 + 1024].rearrange(
                    "p (a s w) -> p a s w", a=2, s=2
                )[:, :, s2, :],
                in_=o.rearrange("p a i c -> p a (i c)"),
            )

        def mx(ch, s2):
            for m in range(4):
                acc = ps_acc.tile([P, 512], F32, name="acc", tag="acc")
                mx_pass(acc, ch, s2, m, 0)
                mx_pass(acc, ch, s2, m, 1)
                leave(acc, ch, s2, m, False)

        pe_path(0)
        pe_path(1)
        for c in range(2):
            nc.scalar.copy(
                out=gg[:, c].rearrange("p (a e) j -> p a j e", e=4),
                in_=g_raw[:, c].rearrange("p j (a e) -> p a j e", e=4),
            )
        def quant_g():
            nc.vector.quantize_mx(
                out=gc.rearrange("p c m -> p (c m)").bitcast(E5X4),
                scales=gs.rearrange("p c m -> p (c m)"),
                in_=gg.rearrange("p c m j -> p (c m j)"),
            )

        for i0, i1 in HEAD:
            st1_plane(0, 0, i0, i1)
            st1_plane(0, 1, i0, i1)
        st1_plane(1, 0, 0, v_i[1])
        st2(0, 0)
        st1_plane(1, 1, 0, v_i[1])
        st2(0, 1)
        pe_path(2)
        pe_path(3)
        st2(1, 0)
        st2(1, 1)
        new_codes(0)
        new_codes(1)
        quant(0, 0, 1024)
        quant(1, 0, 1024)
        for ch in (1, 2):
            k0 = 2 * ch
            k1 = k0 + 1
            st1_plane(k0, 0, 0, v_i[k0])
            st1_plane(k1, 0, 0, v_i[k1])
            if ch == 1:
                quant_g()
                mx(0, 0)
                mx(0, 1)
            st1_plane(k0, 1, 0, v_i[k0])
            st1_plane(k1, 1, 0, v_i[k1])
            pe_path(k0 + 2)
            pe_path(k1 + 2)
            new_codes(k0)
            new_codes(k1)
            for s2 in range(2):
                st2(k0, s2)
                st2(k1, s2)
                quant(k0, 512 * s2, 512 * s2 + 512)
                quant(k1, 512 * s2, 512 * s2 + 512)
                mx(ch, s2)
        assert v_i[7] == 8
        accs = {}

        def open_groups(s2):
            for m in range(4):
                if s2 == 1:
                    acc = ps_acc.tile([P, 512], F32, name="acc", tag="acc")
                elif m < 2:
                    acc = ps_xt.tile([P, 512], F32, name="acc_x", tag="xtp")
                else:
                    acc = ps_hm.tile([P, 512], F32, name="acc_h", tag="hm")
                accs[(s2, m)] = acc
                mx_pass(acc, 3, s2, m, 0)

        def close_groups(s2, share):
            for m in range(4):
                mx_pass(accs[(s2, m)], 3, s2, m, 1)
                leave(accs[(s2, m)], 3, s2, m, share and m % 2 == 1)

        new_codes(6)
        new_codes(7)
        st1_plane(6, 0, 0, v_i[6])
        st1_plane(7, 0, 0, v_i[7])
        st1_plane(6, 1, 0, v_i[6])
        st1_plane(7, 1, 0, v_i[7])
        st2(6, 0)
        st2(7, 0)
        quant(6, 0, 512)
        open_groups(0)
        quant(7, 0, 512)
        close_groups(0, False)
        st2(6, 1)
        st2(7, 1)
        quant(6, 512, 1024)
        open_groups(1)
        quant(7, 768, 1024)
        quant(7, 512, 768)
        close_groups(1, True)
